import numpy as np
import ml_dtypes


def mxq(x, axis, fmt="e4m3"):
    dtype, down = {"e4m3": (ml_dtypes.float8_e4m3fn, 7), "e5m2": (ml_dtypes.float8_e5m2, 14)}[fmt]
    v = np.moveaxis(np.asarray(x, np.float32).astype(ml_dtypes.bfloat16).astype(np.float64), axis, -1)
    blocks = v.reshape(v.shape[:-1] + (-1, 32))
    amax = np.abs(blocks).max(-1, keepdims=True)
    byte = np.maximum(np.where(amax > 0, np.frexp(amax)[1] - 1 + 127, 0) - down, 1)
    scale = np.exp2(byte - 127.0)
    codes = (blocks / scale).astype(np.float32).astype(dtype).astype(np.float64)
    return np.moveaxis((codes * scale).reshape(v.shape), -1, axis)


WIDE = False


def mx_kscale(k):
    if not WIDE:
        return np.ones(k)
    levels = np.array([10, -10, 5, -5, 0])
    a = np.random.permutation(np.resize(levels, k // 512 * 4)).reshape(k // 512, 4)
    idx = np.arange(k)
    return np.exp2(a[idx // 512, idx % 128 // 32])


BF16 = ml_dtypes.bfloat16


def bf(x):
    return np.asarray(x, np.float32).astype(BF16)


def f64(x):
    return np.asarray(x).astype(np.float64)


B, SD, A, H, HS, M, C, F1, F2 = 1024, 896, 128, 1024, 32, 896, 2, 2048, 300
K2 = M + A
EPS = 1e-12


def l2norm(v):
    n = np.sqrt(np.sum(v * v, axis=-1, keepdims=True))
    return v / np.maximum(n, EPS)


def setup_inputs():
    s = mx_kscale(H)
    t = mx_kscale(K2)[M:]
    col = np.concatenate([np.full(M, 0.7), 0.7 / np.sqrt(A) / t])
    return {"xum": bf(np.tanh(np.random.standard_normal((B, H))) * s),
            "action": bf(np.random.standard_normal((B, A)) * t),
            "up_w3": bf(np.random.standard_normal((M, H)) * 1.5 / np.sqrt(H) / s[None, :]),
            "up_b3": bf(np.random.standard_normal(M) * 0.3),
            "dyn_w1_mu": bf(np.random.standard_normal((F1, K2)) * col[None, :]),
            "dyn_b1": bf(np.random.standard_normal(F1) * 0.3)}


def reference(xum, action, up_w3, up_b3, dyn_w1_mu, dyn_b1):
    msg_up = l2norm((mxq(f64(xum), 1, "e4m3") @ mxq(f64(up_w3), 1, "e4m3").T) + f64(up_b3))
    mu = np.concatenate([msg_up, f64(action)], axis=-1)
    return np.maximum((mxq(mu, 1, "e4m3") @ mxq(f64(dyn_w1_mu), 1, "e4m3").T) + f64(dyn_b1), 0.0)

@@ -1,0 +1,229 @@
+import math
+from contextlib import ExitStack
+
+import concourse.mybir as mybir
+from concourse.masks import make_identity
+
+F32 = mybir.dt.float32
+BF16 = mybir.dt.bfloat16
+U32 = mybir.dt.uint32
+U8 = mybir.dt.uint8
+FP8X4 = mybir.dt.float8_e4m3fn_x4
+ACT = mybir.ActivationFunctionType
+ALU = mybir.AluOpType
+
+P = 128
+PACK = 4
+PAIRS = 2
+K = 1024
+PASSES = K // (P * PACK)
+BANK = 512
+
+BATCH = 1024
+MESSAGE = 896
+ACTION = K - MESSAGE
+OUT = 2048
+EPS = 1e-12
+
+B_TILES = BATCH // P
+GROUP = BANK // P
+X_GROUPS = B_TILES // GROUP
+W1_GROUPS = OUT // BANK
+W3_GROUP_TILES = (4, 2, 1)
+W3_GROUP_START = (0, 512, 768)
+
+WORDS_IN_HALVES = "r (j g u p) -> r j g u p"
+WORDS_IN_TURN = "r (j g p u) -> r j g u p"
+
+LAG = W1_GROUPS
+
+FLOPS = 2 * BATCH * K * (MESSAGE + OUT)
+
+
+def load_rows(nc, pool, rows, name):
+    n_tiles = rows.shape[0] // P
+    rows_sb = pool.tile([P, n_tiles * K], BF16, name=name)
+    nc.sync.dma_start(
+        out=rows_sb[:].rearrange("r (j k) -> r j k", j=n_tiles),
+        in_=rows.rearrange("(j r) k -> r j k", r=P),
+    )
+    return rows_sb
+
+
+def quantise_rows(nc, pools, identity, rows_sb, word_order, name):
+    n_rows = rows_sb.shape[1] // K * P
+    words = rows_sb[:].bitcast(F32).rearrange(word_order, j=n_rows // P, g=PASSES, u=PAIRS, p=P)
+    codes = pools["operands"].tile([P, PASSES, n_rows], U32, name=name + "_codes", align_bytes=64)
+    scales = pools["operands"].tile([P, PASSES, n_rows], U8, name=name + "_scales", align_bytes=64)
+    grouped = pools["grouped"].tile([P, PASSES * n_rows * PACK], BF16, tag="grouped", align_bytes=64)
+    grouped_words = grouped[:].bitcast(F32).rearrange("p (g r u) -> p g r u", g=PASSES, u=PAIRS)
+    for j in range(n_rows // P):
+        flipped = pools["psum"].tile([P, PASSES, PAIRS, P], F32, tag="bank")
+        for g in range(PASSES):
+            for u in range(PAIRS):
+                nc.tensor.transpose(flipped[:, g, u, :], words[:, j, g, u, :], identity[:])
+        copy = nc.scalar.copy if j % 2 == 0 else nc.vector.tensor_copy
+        copy(
+            out=grouped_words[:, :, j * P : (j + 1) * P, :],
+            in_=flipped[:].rearrange("p g u r -> p g r u"),
+        )
+    width = n_rows * PACK
+    for g in range(PASSES):
+        nc.vector.quantize_mx(
+            out=codes[:, g, :].bitcast(FP8X4),
+            scales=scales[:, g, :],
+            in_=grouped[:, g * width : (g + 1) * width],
+        )
+    return codes, scales
+
+
+def tile_modelgraphpolicy_pb_kernel(tc, xum, action, up_w3, up_b3, dyn_w1_mu, dyn_b1, out):
+    nc = tc.nc
+    with ExitStack() as ctx:
+        const = ctx.enter_context(tc.tile_pool(name="const", bufs=1))
+        raw = ctx.enter_context(tc.tile_pool(name="raw", bufs=1))
+        work = ctx.enter_context(tc.tile_pool(name="work", bufs=3))
+        small = ctx.enter_context(tc.tile_pool(name="small", bufs=3))
+        pools = {
+            "operands": ctx.enter_context(tc.tile_pool(name="operands", bufs=1)),
+            "grouped": ctx.enter_context(tc.tile_pool(name="grouped", bufs=3)),
+            "psum": ctx.enter_context(tc.psum_pool(name="psum", bufs=8)),
+        }
+        psum = pools["psum"]
+
+        b3_all = const.tile([P, MESSAGE], BF16)
+        nc.gpsimd.dma_start(out=b3_all[:], in_=up_b3.partition_broadcast(P))
+        action_sb = raw.tile([P, B_TILES, ACTION], BF16)
+        nc.scalar.dma_start(out=action_sb[:], in_=action.rearrange("(i b) a -> b i a", b=P))
+        x_rows = [load_rows(nc, raw, xum[0 : BANK, :], "x_rows0")]
+        w3_rows = [
+            load_rows(nc, raw, up_w3[start : start + tiles * P, :], "w3_rows%d" % start)
+            for start, tiles in zip(W3_GROUP_START, W3_GROUP_TILES)
+        ]
+        x_rows.append(load_rows(nc, raw, xum[BANK : 2 * BANK, :], "x_rows1"))
+        w1_rows = [
+            load_rows(nc, raw, dyn_w1_mu[n * BANK : (n + 1) * BANK, :], "w1_rows%d" % n)
+            for n in range(W1_GROUPS)
+        ]
+        b1_all = const.tile([P, OUT], BF16)
+        nc.sync.dma_start(out=b1_all[:], in_=dyn_b1.partition_broadcast(P))
+
+        identity_f32 = const.tile([P, P], F32)
+        make_identity(nc, identity_f32[:])
+        identity_bf16 = const.tile([P, P], BF16)
+        make_identity(nc, identity_bf16[:])
+        one = const.tile([P, 1], F32)
+        nc.vector.memset(one[:], 1.0)
+        nc.scalar.sqrt(one[:], one[:])
+
+        mu_planes = raw.tile([P, B_TILES, PASSES, PACK, P], BF16)
+        message_p = (MESSAGE - P * PACK) // PACK
+        nc.vector.tensor_copy(
+            out=mu_planes[:, :, 1, :, message_p:P],
+            in_=action_sb[:].rearrange("b i (p t) -> b i t p", t=PACK),
+        )
+        mu_codes = pools["operands"].tile([P, B_TILES, PASSES, P], U32, align_bytes=64)
+        mu_scales = pools["operands"].tile([P, B_TILES, PASSES, P], U8, align_bytes=64)
+
+        x_ops = [quantise_rows(nc, pools, identity_f32, x_rows[0], WORDS_IN_HALVES, "x0")]
+        w3_ops = [
+            quantise_rows(nc, pools, identity_f32, rows_sb, WORDS_IN_HALVES, "w3_%d" % start)
+            for rows_sb, start in zip(w3_rows, W3_GROUP_START)
+        ]
+        x_ops.append(quantise_rows(nc, pools, identity_f32, x_rows[1], WORDS_IN_HALVES, "x1"))
+        w1_ops = []
+
+        def first_layer(i):
+            x_codes, x_scales = x_ops[i // GROUP]
+            b_cols = slice((i % GROUP) * P, (i % GROUP + 1) * P)
+            z_ps = [psum.tile([P, BANK], F32, tag="bank", name="z_ps%d" % h) for h in range(2)]
+            for (w3_codes, w3_scales), start in zip(w3_ops, W3_GROUP_START):
+                width = w3_codes.shape[2]
+                for g in range(PASSES):
+                    nc.tensor.matmul_mx(
+                        out=z_ps[start // BANK][:, start % BANK : start % BANK + width],
+                        lhsT=x_codes[:, g, b_cols].bitcast(FP8X4),
+                        lhsT_scale=x_scales[:, g, b_cols],
+                        rhs=w3_codes[:, g, :].bitcast(FP8X4),
+                        rhs_scale=w3_scales[:, g, :],
+                        start=(g == 0),
+                        stop=(g == PASSES - 1),
+                    )
+            z = work.tile([P, MESSAGE], F32, tag="z")
+            nc.vector.tensor_tensor(out=z[:, 0:BANK], in0=z_ps[0][:], in1=b3_all[:, 0:BANK], op=ALU.add)
+            nc.vector.tensor_tensor(
+                out=z[:, BANK:MESSAGE],
+                in0=z_ps[1][:, 0 : MESSAGE - BANK],
+                in1=b3_all[:, BANK:MESSAGE],
+                op=ALU.add,
+            )
+            squares = work.tile([P, MESSAGE], F32, tag="squares")
+            sum_squares = small.tile([P, 1], F32, tag="sum_squares")
+            nc.scalar.activation(out=squares[:], in_=z[:], func=ACT.Square, accum_out=sum_squares[:])
+            norm = small.tile([P, 1], F32, tag="norm")
+            nc.scalar.sqrt(norm[:], sum_squares[:])
+            floored = small.tile([P, 1], F32, tag="floored")
+            nc.vector.tensor_scalar_max(floored[:], norm[:], EPS)
+            inverse = small.tile([P, 1], F32, tag="inverse")
+            nc.vector.reciprocal(inverse[:], floored[:])
+            for g, first, last in ((0, 0, P * PACK), (1, P * PACK, MESSAGE)):
+                nc.scalar.activation(
+                    out=mu_planes[:, i, g, :, 0 : (last - first) // PACK].rearrange("b t p -> b p t"),
+                    in_=z[:, first:last].rearrange("b (p t) -> b p t", t=PACK),
+                    func=ACT.Copy,
+                    scale=inverse[:],
+                )
+
+        def quantise_mu(i):
+            flipped = psum.tile([P, PASSES, PACK, P], BF16, tag="bank")
+            for g in range(PASSES):
+                for t in range(PACK):
+                    nc.tensor.transpose(flipped[:, g, t, :], mu_planes[:, i, g, t, :], identity_bf16[:])
+            grouped = work.tile([P, PASSES, P, PACK], BF16, tag="mu_grouped", align_bytes=64)
+            nc.scalar.copy(out=grouped[:], in_=flipped[:].rearrange("p g t b -> p g b t"))
+            nc.vector.quantize_mx(
+                out=mu_codes[:, i].rearrange("p g b -> p (g b)").bitcast(FP8X4),
+                scales=mu_scales[:, i].rearrange("p g b -> p (g b)"),
+                in_=grouped[:].rearrange("p g b t -> p (g b t)"),
+            )
+
+        def second_layer(i):
+            result = work.tile([P, OUT], F32, tag="result")
+            for n, (w1_codes, w1_scales) in enumerate(w1_ops):
+                n_cols = slice(n * BANK, (n + 1) * BANK)
+                acc = psum.tile([P, BANK], F32, tag="bank")
+                for g in range(PASSES):
+                    nc.tensor.matmul_mx(
+                        out=acc[:],
+                        lhsT=mu_codes[:, i, g, :].bitcast(FP8X4),
+                        lhsT_scale=mu_scales[:, i, g, :],
+                        rhs=w1_codes[:, g, :].bitcast(FP8X4),
+                        rhs_scale=w1_scales[:, g, :],
+                        start=(g == 0),
+                        stop=(g == PASSES - 1),
+                    )
+                nc.vector.tensor_tensor(out=result[:, n_cols], in0=acc[:], in1=b1_all[:, n_cols], op=ALU.add)
+            rows = slice(i * P, (i + 1) * P)
+            for first in range(0, OUT, OUT // 2):
+                half = slice(first, first + OUT // 2)
+                nc.gpsimd.tensor_scalar(
+                    out=result[:, half],
+                    in0=result[:, half],
+                    scalar1=math.inf,
+                    scalar2=0.0,
+                    op0=ALU.min,
+                    op1=ALU.max,
+                )
+                nc.sync.dma_start(out=out[rows, half], in_=result[:, half])
+
+        for step in range(B_TILES + LAG):
+            if step < B_TILES:
+                first_layer(step)
+            if 1 <= step <= B_TILES:
+                quantise_mu(step - 1)
+            if step < W1_GROUPS:
+                w1_ops.append(
+                    quantise_rows(nc, pools, identity_f32, w1_rows[step], WORDS_IN_TURN, "w1_%d" % step)
+                )
+            if step >= LAG:
+                second_layer(step - LAG)

@@ -27,7 +27,6 @@ EPS = 1e-12
 
 B_TILES = BATCH // P
 GROUP = BANK // P
-X_GROUPS = B_TILES // GROUP
 W1_GROUPS = OUT // BANK
 W3_GROUP_TILES = (4, 2, 1)
 W3_GROUP_START = (0, 512, 768)
@@ -50,31 +49,39 @@ def load_rows(nc, pool, rows, name):
     return rows_sb
 
 
-def quantise_rows(nc, pools, identity, rows_sb, word_order, name):
+def new_group(pools, rows_sb, word_order, name):
     n_rows = rows_sb.shape[1] // K * P
-    words = rows_sb[:].bitcast(F32).rearrange(word_order, j=n_rows // P, g=PASSES, u=PAIRS, p=P)
-    codes = pools["operands"].tile([P, PASSES, n_rows], U32, name=name + "_codes", align_bytes=64)
-    scales = pools["operands"].tile([P, PASSES, n_rows], U8, name=name + "_scales", align_bytes=64)
     grouped = pools["grouped"].tile([P, PASSES * n_rows * PACK], BF16, tag="grouped", align_bytes=64)
-    grouped_words = grouped[:].bitcast(F32).rearrange("p (g r u) -> p g r u", g=PASSES, u=PAIRS)
-    for j in range(n_rows // P):
-        flipped = pools["psum"].tile([P, PASSES, PAIRS, P], F32, tag="bank")
-        for g in range(PASSES):
-            for u in range(PAIRS):
-                nc.tensor.transpose(flipped[:, g, u, :], words[:, j, g, u, :], identity[:])
-        copy = nc.scalar.copy if j % 2 == 0 else nc.vector.tensor_copy
-        copy(
-            out=grouped_words[:, :, j * P : (j + 1) * P, :],
-            in_=flipped[:].rearrange("p g u r -> p g r u"),
-        )
-    width = n_rows * PACK
+    return {
+        "n_tiles": n_rows // P,
+        "words": rows_sb[:].bitcast(F32).rearrange(word_order, j=n_rows // P, g=PASSES, u=PAIRS, p=P),
+        "grouped": grouped,
+        "grouped_words": grouped[:].bitcast(F32).rearrange("p (g r u) -> p g r u", g=PASSES, u=PAIRS),
+        "codes": pools["operands"].tile([P, PASSES, n_rows], U32, name=name + "_codes", align_bytes=64),
+        "scales": pools["operands"].tile([P, PASSES, n_rows], U8, name=name + "_scales", align_bytes=64),
+    }
+
+
+def flip_row_tile(nc, pools, identity, group, j):
+    flipped = pools["psum"].tile([P, PASSES, PAIRS, P], F32, tag="bank")
+    for g in range(PASSES):
+        for u in range(PAIRS):
+            nc.tensor.transpose(flipped[:, g, u, :], group["words"][:, j, g, u, :], identity[:])
+    copy = nc.scalar.copy if j % 2 == 0 else nc.vector.tensor_copy
+    copy(
+        out=group["grouped_words"][:, :, j * P : (j + 1) * P, :],
+        in_=flipped[:].rearrange("p g u r -> p g r u"),
+    )
+
+
+def quantise_group(nc, group):
+    width = group["n_tiles"] * P * PACK
     for g in range(PASSES):
         nc.vector.quantize_mx(
-            out=codes[:, g, :].bitcast(FP8X4),
-            scales=scales[:, g, :],
-            in_=grouped[:, g * width : (g + 1) * width],
+            out=group["codes"][:, g, :].bitcast(FP8X4),
+            scales=group["scales"][:, g, :],
+            in_=group["grouped"][:, g * width : (g + 1) * width],
         )
-    return codes, scales
 
 
 def tile_modelgraphpolicy_pb_kernel(tc, xum, action, up_w3, up_b3, dyn_w1_mu, dyn_b1, out):
@@ -84,18 +91,20 @@ def tile_modelgraphpolicy_pb_kernel(tc, xum, action, up_w3, up_b3, dyn_w1_mu, dy
         raw = ctx.enter_context(tc.tile_pool(name="raw", bufs=1))
         work = ctx.enter_context(tc.tile_pool(name="work", bufs=3))
         small = ctx.enter_context(tc.tile_pool(name="small", bufs=3))
+        results = ctx.enter_context(tc.tile_pool(name="results", bufs=6))
         pools = {
             "operands": ctx.enter_context(tc.tile_pool(name="operands", bufs=1)),
             "grouped": ctx.enter_context(tc.tile_pool(name="grouped", bufs=3)),
             "psum": ctx.enter_context(tc.psum_pool(name="psum", bufs=8)),
         }
         psum = pools["psum"]
+        ctx.enter_context(tc.manual_schedule())
 
         b3_all = const.tile([P, MESSAGE], BF16)
         nc.gpsimd.dma_start(out=b3_all[:], in_=up_b3.partition_broadcast(P))
         action_sb = raw.tile([P, B_TILES, ACTION], BF16)
         nc.scalar.dma_start(out=action_sb[:], in_=action.rearrange("(i b) a -> b i a", b=P))
-        x_rows = [load_rows(nc, raw, xum[0 : BANK, :], "x_rows0")]
+        x_rows = [load_rows(nc, raw, xum[0:BANK, :], "x_rows0")]
         w3_rows = [
             load_rows(nc, raw, up_w3[start : start + tiles * P, :], "w3_rows%d" % start)
             for start, tiles in zip(W3_GROUP_START, W3_GROUP_TILES)
@@ -125,105 +134,155 @@ def tile_modelgraphpolicy_pb_kernel(tc, xum, action, up_w3, up_b3, dyn_w1_mu, dy
         mu_codes = pools["operands"].tile([P, B_TILES, PASSES, P], U32, align_bytes=64)
         mu_scales = pools["operands"].tile([P, B_TILES, PASSES, P], U8, align_bytes=64)
 
-        x_ops = [quantise_rows(nc, pools, identity_f32, x_rows[0], WORDS_IN_HALVES, "x0")]
-        w3_ops = [
-            quantise_rows(nc, pools, identity_f32, rows_sb, WORDS_IN_HALVES, "w3_%d" % start)
-            for rows_sb, start in zip(w3_rows, W3_GROUP_START)
-        ]
-        x_ops.append(quantise_rows(nc, pools, identity_f32, x_rows[1], WORDS_IN_HALVES, "x1"))
-        w1_ops = []
+        first_groups = []
+        for rows_sb, name in zip([x_rows[0]] + w3_rows + [x_rows[1]], ["x0", "w3_0", "w3_1", "w3_2", "x1"]):
+            group = new_group(pools, rows_sb, WORDS_IN_HALVES, name)
+            for j in range(group["n_tiles"]):
+                flip_row_tile(nc, pools, identity_f32, group, j)
+            quantise_group(nc, group)
+            first_groups.append(group)
+        x_groups = [first_groups[0], first_groups[-1]]
+        w3_groups = first_groups[1:-1]
+        w1_groups = []
 
-        def first_layer(i):
-            x_codes, x_scales = x_ops[i // GROUP]
+        z_ps, z, norm, inverse, mu_flipped, mu_grouped = {}, {}, {}, {}, {}, {}
+
+        def first_matmul(i):
+            x = x_groups[i // GROUP]
             b_cols = slice((i % GROUP) * P, (i % GROUP + 1) * P)
-            z_ps = [psum.tile([P, BANK], F32, tag="bank", name="z_ps%d" % h) for h in range(2)]
-            for (w3_codes, w3_scales), start in zip(w3_ops, W3_GROUP_START):
-                width = w3_codes.shape[2]
+            z_ps[i] = [psum.tile([P, BANK], F32, tag="bank", name="z_ps%d" % h) for h in range(2)]
+            for w3, start in zip(w3_groups, W3_GROUP_START):
+                width = w3["n_tiles"] * P
                 for g in range(PASSES):
                     nc.tensor.matmul_mx(
-                        out=z_ps[start // BANK][:, start % BANK : start % BANK + width],
-                        lhsT=x_codes[:, g, b_cols].bitcast(FP8X4),
-                        lhsT_scale=x_scales[:, g, b_cols],
-                        rhs=w3_codes[:, g, :].bitcast(FP8X4),
-                        rhs_scale=w3_scales[:, g, :],
+                        out=z_ps[i][start // BANK][:, start % BANK : start % BANK + width],
+                        lhsT=x["codes"][:, g, b_cols].bitcast(FP8X4),
+                        lhsT_scale=x["scales"][:, g, b_cols],
+                        rhs=w3["codes"][:, g, :].bitcast(FP8X4),
+                        rhs_scale=w3["scales"][:, g, :],
                         start=(g == 0),
                         stop=(g == PASSES - 1),
                     )
-            z = work.tile([P, MESSAGE], F32, tag="z")
-            nc.vector.tensor_tensor(out=z[:, 0:BANK], in0=z_ps[0][:], in1=b3_all[:, 0:BANK], op=ALU.add)
+
+        def add_first_bias(i):
+            z[i] = work.tile([P, MESSAGE], F32, tag="z", name="z")
             nc.vector.tensor_tensor(
-                out=z[:, BANK:MESSAGE],
-                in0=z_ps[1][:, 0 : MESSAGE - BANK],
+                out=z[i][:, 0:BANK], in0=z_ps[i][0][:], in1=b3_all[:, 0:BANK], op=ALU.add
+            )
+            nc.vector.tensor_tensor(
+                out=z[i][:, BANK:MESSAGE],
+                in0=z_ps[i][1][:, 0 : MESSAGE - BANK],
                 in1=b3_all[:, BANK:MESSAGE],
                 op=ALU.add,
             )
+
+        def take_norm(i):
             squares = work.tile([P, MESSAGE], F32, tag="squares")
             sum_squares = small.tile([P, 1], F32, tag="sum_squares")
-            nc.scalar.activation(out=squares[:], in_=z[:], func=ACT.Square, accum_out=sum_squares[:])
-            norm = small.tile([P, 1], F32, tag="norm")
-            nc.scalar.sqrt(norm[:], sum_squares[:])
+            nc.scalar.activation(out=squares[:], in_=z[i][:], func=ACT.Square, accum_out=sum_squares[:])
+            norm[i] = small.tile([P, 1], F32, tag="norm", name="norm")
+            nc.scalar.sqrt(norm[i][:], sum_squares[:])
+
+        def invert_norm(i):
             floored = small.tile([P, 1], F32, tag="floored")
-            nc.vector.tensor_scalar_max(floored[:], norm[:], EPS)
-            inverse = small.tile([P, 1], F32, tag="inverse")
-            nc.vector.reciprocal(inverse[:], floored[:])
+            nc.vector.tensor_scalar_max(floored[:], norm[i][:], EPS)
+            inverse[i] = small.tile([P, 1], F32, tag="inverse", name="inverse")
+            nc.vector.reciprocal(inverse[i][:], floored[:])
+
+        def round_message(i):
             for g, first, last in ((0, 0, P * PACK), (1, P * PACK, MESSAGE)):
                 nc.scalar.activation(
                     out=mu_planes[:, i, g, :, 0 : (last - first) // PACK].rearrange("b t p -> b p t"),
-                    in_=z[:, first:last].rearrange("b (p t) -> b p t", t=PACK),
+                    in_=z[i][:, first:last].rearrange("b (p t) -> b p t", t=PACK),
                     func=ACT.Copy,
-                    scale=inverse[:],
+                    scale=inverse[i][:],
                 )
 
-        def quantise_mu(i):
-            flipped = psum.tile([P, PASSES, PACK, P], BF16, tag="bank")
+        def flip_mu(i):
+            mu_flipped[i] = psum.tile([P, PASSES, PACK, P], BF16, tag="bank", name="mu_flipped")
             for g in range(PASSES):
                 for t in range(PACK):
-                    nc.tensor.transpose(flipped[:, g, t, :], mu_planes[:, i, g, t, :], identity_bf16[:])
-            grouped = work.tile([P, PASSES, P, PACK], BF16, tag="mu_grouped", align_bytes=64)
-            nc.scalar.copy(out=grouped[:], in_=flipped[:].rearrange("p g t b -> p g b t"))
+                    nc.tensor.transpose(
+                        mu_flipped[i][:, g, t, :], mu_planes[:, i, g, t, :], identity_bf16[:]
+                    )
+
+        def group_mu(i):
+            mu_grouped[i] = work.tile(
+                [P, PASSES, P, PACK], BF16, tag="mu_grouped", name="mu_grouped", align_bytes=64
+            )
+            nc.scalar.copy(out=mu_grouped[i][:], in_=mu_flipped[i][:].rearrange("p g t b -> p g b t"))
+
+        def quantise_mu(i):
             nc.vector.quantize_mx(
                 out=mu_codes[:, i].rearrange("p g b -> p (g b)").bitcast(FP8X4),
                 scales=mu_scales[:, i].rearrange("p g b -> p (g b)"),
-                in_=grouped[:].rearrange("p g b t -> p (g b t)"),
+                in_=mu_grouped[i][:].rearrange("p g b t -> p (g b t)"),
             )
 
-        def second_layer(i):
-            result = work.tile([P, OUT], F32, tag="result")
-            for n, (w1_codes, w1_scales) in enumerate(w1_ops):
-                n_cols = slice(n * BANK, (n + 1) * BANK)
-                acc = psum.tile([P, BANK], F32, tag="bank")
-                for g in range(PASSES):
-                    nc.tensor.matmul_mx(
-                        out=acc[:],
-                        lhsT=mu_codes[:, i, g, :].bitcast(FP8X4),
-                        lhsT_scale=mu_scales[:, i, g, :],
-                        rhs=w1_codes[:, g, :].bitcast(FP8X4),
-                        rhs_scale=w1_scales[:, g, :],
-                        start=(g == 0),
-                        stop=(g == PASSES - 1),
-                    )
-                nc.vector.tensor_tensor(out=result[:, n_cols], in0=acc[:], in1=b1_all[:, n_cols], op=ALU.add)
-            rows = slice(i * P, (i + 1) * P)
-            for first in range(0, OUT, OUT // 2):
-                half = slice(first, first + OUT // 2)
-                nc.gpsimd.tensor_scalar(
-                    out=result[:, half],
-                    in0=result[:, half],
-                    scalar1=math.inf,
-                    scalar2=0.0,
-                    op0=ALU.min,
-                    op1=ALU.max,
+        def link(stage, i):
+            if 0 <= i < B_TILES:
+                stage(i)
+
+        result = {}
+
+        def second_matmul(i, n):
+            w1 = w1_groups[n]
+            acc = psum.tile([P, BANK], F32, tag="bank")
+            for g in range(PASSES):
+                nc.tensor.matmul_mx(
+                    out=acc[:],
+                    lhsT=mu_codes[:, i, g, :].bitcast(FP8X4),
+                    lhsT_scale=mu_scales[:, i, g, :],
+                    rhs=w1["codes"][:, g, :].bitcast(FP8X4),
+                    rhs_scale=w1["scales"][:, g, :],
+                    start=(g == 0),
+                    stop=(g == PASSES - 1),
                 )
-                nc.sync.dma_start(out=out[rows, half], in_=result[:, half])
+            side = n % 2
+            if side == 0:
+                result[i] = results.tile([P, 2 * BANK], F32, tag="result", name="result")
+            nc.vector.tensor_tensor(
+                out=result[i][:, side * BANK : (side + 1) * BANK],
+                in0=acc[:],
+                in1=b1_all[:, n * BANK : (n + 1) * BANK],
+                op=ALU.add,
+            )
+            if side == 1:
+                if i < LAG:
+                    nc.gpsimd.tensor_scalar(
+                        out=result[i][:],
+                        in0=result[i][:],
+                        scalar1=math.inf,
+                        scalar2=0.0,
+                        op0=ALU.min,
+                        op1=ALU.max,
+                    )
+                else:
+                    nc.scalar.activation(out=result[i][:], in_=result[i][:], func=ACT.Relu)
+                nc.sync.dma_start(
+                    out=out[i * P : (i + 1) * P, (n - 1) * BANK : (n + 1) * BANK], in_=result[i][:]
+                )
+
+        def bulk_quarter(step, quarter):
+            if step < W1_GROUPS:
+                if quarter == 0:
+                    w1_groups.append(new_group(pools, w1_rows[step], WORDS_IN_TURN, "w1_%d" % step))
+                flip_row_tile(nc, pools, identity_f32, w1_groups[step], quarter)
+                if quarter == GROUP - 1:
+                    quantise_group(nc, w1_groups[step])
+            if step >= LAG:
+                second_matmul(step - LAG, quarter)
 
         for step in range(B_TILES + LAG):
-            if step < B_TILES:
-                first_layer(step)
-            if 1 <= step <= B_TILES:
-                quantise_mu(step - 1)
-            if step < W1_GROUPS:
-                w1_ops.append(
-                    quantise_rows(nc, pools, identity_f32, w1_rows[step], WORDS_IN_TURN, "w1_%d" % step)
-                )
-            if step >= LAG:
-                second_layer(step - LAG)
+            link(invert_norm, step - 1)
+            link(flip_mu, step - 2)
+            link(first_matmul, step)
+            bulk_quarter(step, 0)
+            link(round_message, step - 1)
+            link(add_first_bias, step)
+            bulk_quarter(step, 1)
+            link(group_mu, step - 2)
+            link(quantise_mu, step - 3)
+            bulk_quarter(step, 2)
+            link(take_norm, step)
+            bulk_quarter(step, 3)

@@ -191,12 +191,19 @@ def tile_modelgraphpolicy_pb_kernel(tc, xum, action, up_w3, up_b3, dyn_w1_mu, dy
 
         def round_message(i):
             for g, first, last in ((0, 0, P * PACK), (1, P * PACK, MESSAGE)):
-                nc.scalar.activation(
-                    out=mu_planes[:, i, g, :, 0 : (last - first) // PACK].rearrange("b t p -> b p t"),
-                    in_=z[i][:, first:last].rearrange("b (p t) -> b p t", t=PACK),
-                    func=ACT.Copy,
-                    scale=inverse[i][:],
-                )
+                planes = mu_planes[:, i, g, :, 0 : (last - first) // PACK].rearrange("b t p -> b p t")
+                columns = z[i][:, first:last].rearrange("b (p t) -> b p t", t=PACK)
+                if i < LAG:
+                    nc.gpsimd.tensor_scalar(
+                        out=planes,
+                        in0=columns,
+                        scalar1=inverse[i][:],
+                        scalar2=0.0,
+                        op0=ALU.mult,
+                        op1=ALU.add,
+                    )
+                else:
+                    nc.scalar.activation(out=planes, in_=columns, func=ACT.Copy, scale=inverse[i][:])
 
         def flip_mu(i):
             mu_flipped[i] = psum.tile([P, PASSES, PACK, P], BF16, tag="bank", name="mu_flipped")

@@ -8,6 +8,7 @@ F32 = mybir.dt.float32
 BF16 = mybir.dt.bfloat16
 U32 = mybir.dt.uint32
 U8 = mybir.dt.uint8
+I32 = mybir.dt.int32
 FP8X4 = mybir.dt.float8_e4m3fn_x4
 ACT = mybir.ActivationFunctionType
 ALU = mybir.AluOpType
@@ -31,6 +32,12 @@ W1_GROUPS = OUT // BANK
 W3_GROUP_TILES = (4, 2, 1)
 W3_GROUP_START = (0, 512, 768)
 
+ROWS_APART = "(j r) k -> r j k"
+ROWS_TOGETHER = "(r j) k -> r j k"
+
+B1_START = 2 * BANK
+BIAS_COLUMNS = B1_START + OUT
+
 WORDS_IN_HALVES = "r (j g u p) -> r j g u p"
 WORDS_IN_TURN = "r (j g p u) -> r j g u p"
 
@@ -39,12 +46,12 @@ LAG = W1_GROUPS
 FLOPS = 2 * BATCH * K * (MESSAGE + OUT)
 
 
-def load_rows(nc, pool, rows, name):
+def load_rows(nc, pool, rows, row_order, name):
     n_tiles = rows.shape[0] // P
     rows_sb = pool.tile([P, n_tiles * K], BF16, name=name)
     nc.sync.dma_start(
         out=rows_sb[:].rearrange("r (j k) -> r j k", j=n_tiles),
-        in_=rows.rearrange("(j r) k -> r j k", r=P),
+        in_=rows.rearrange(row_order, r=P),
     )
     return rows_sb
 
@@ -67,7 +74,7 @@ def flip_row_tile(nc, pools, identity, group, j):
     for g in range(PASSES):
         for u in range(PAIRS):
             nc.tensor.transpose(flipped[:, g, u, :], group["words"][:, j, g, u, :], identity[:])
-    copy = nc.scalar.copy if j % 2 == 0 else nc.vector.tensor_copy
+    copy = nc.vector.tensor_copy if j == 1 else nc.scalar.copy
     copy(
         out=group["grouped_words"][:, :, j * P : (j + 1) * P, :],
         in_=flipped[:].rearrange("p g u r -> p g r u"),
@@ -100,22 +107,26 @@ def tile_modelgraphpolicy_pb_kernel(tc, xum, action, up_w3, up_b3, dyn_w1_mu, dy
         psum = pools["psum"]
         ctx.enter_context(tc.manual_schedule())
 
-        b3_all = const.tile([P, MESSAGE], BF16)
-        nc.gpsimd.dma_start(out=b3_all[:], in_=up_b3.partition_broadcast(P))
-        action_sb = raw.tile([P, B_TILES, ACTION], BF16)
-        nc.scalar.dma_start(out=action_sb[:], in_=action.rearrange("(i b) a -> b i a", b=P))
-        x_rows = [load_rows(nc, raw, xum[0:BANK, :], "x_rows0")]
+        bias_rows = const.tile([P, BIAS_COLUMNS], BF16)
+        nc.vector.memset(bias_rows[:].bitcast(I32), 0)
+        nc.scalar.dma_start(out=bias_rows[0:1, 0:MESSAGE], in_=up_b3.unsqueeze(0))
+        nc.scalar.dma_start(out=bias_rows[0:1, B1_START:BIAS_COLUMNS], in_=dyn_b1.unsqueeze(0))
+        x_rows = [load_rows(nc, raw, xum[0:BANK, :], ROWS_TOGETHER, "x_rows0")]
         w3_rows = [
-            load_rows(nc, raw, up_w3[start : start + tiles * P, :], "w3_rows%d" % start)
+            load_rows(nc, raw, up_w3[start : start + tiles * P, :], ROWS_APART, "w3_rows%d" % start)
             for start, tiles in zip(W3_GROUP_START, W3_GROUP_TILES)
         ]
-        x_rows.append(load_rows(nc, raw, xum[BANK : 2 * BANK, :], "x_rows1"))
+        x_rows.append(load_rows(nc, raw, xum[BANK : 2 * BANK, :], ROWS_TOGETHER, "x_rows1"))
+        action_sb = raw.tile([P, B_TILES, ACTION], BF16)
+        nc.sync.dma_start(
+            out=action_sb[:].rearrange("r (h j) a -> r h j a", j=GROUP),
+            in_=action.rearrange("(h r j) a -> r h j a", r=P, j=GROUP),
+        )
         w1_rows = [
-            load_rows(nc, raw, dyn_w1_mu[n * BANK : (n + 1) * BANK, :], "w1_rows%d" % n)
+            load_rows(nc, raw, dyn_w1_mu[n * BANK : (n + 1) * BANK, :], ROWS_APART, "w1_rows%d" % n)
             for n in range(W1_GROUPS)
         ]
-        b1_all = const.tile([P, OUT], BF16)
-        nc.sync.dma_start(out=b1_all[:], in_=dyn_b1.partition_broadcast(P))
+        out_tiles = out.rearrange("(h r j) n -> h j r n", r=P, j=GROUP)
 
         identity_f32 = const.tile([P, P], F32)
         make_identity(nc, identity_f32[:])
@@ -125,24 +136,33 @@ def tile_modelgraphpolicy_pb_kernel(tc, xum, action, up_w3, up_b3, dyn_w1_mu, dy
         nc.vector.memset(one[:], 1.0)
         nc.scalar.sqrt(one[:], one[:])
 
+        ones = const.tile([P, P], BF16)
+        nc.vector.memset(ones[:], 1.0)
+        bias_all = const.tile([P, BIAS_COLUMNS], BF16)
+
+        def spread_bias(piece):
+            columns = slice(piece * BANK, (piece + 1) * BANK)
+            spread = psum.tile([P, BANK], F32, tag="bank")
+            nc.tensor.matmul(out=spread[:], lhsT=ones[:], rhs=bias_rows[:, columns], start=True, stop=True)
+            nc.scalar.copy(out=bias_all[:, columns], in_=spread[:])
+
         mu_planes = raw.tile([P, B_TILES, PASSES, PACK, P], BF16)
         message_p = (MESSAGE - P * PACK) // PACK
-        nc.vector.tensor_copy(
-            out=mu_planes[:, :, 1, :, message_p:P],
-            in_=action_sb[:].rearrange("b i (p t) -> b i t p", t=PACK),
-        )
         mu_codes = pools["operands"].tile([P, B_TILES, PASSES, P], U32, align_bytes=64)
         mu_scales = pools["operands"].tile([P, B_TILES, PASSES, P], U8, align_bytes=64)
 
-        first_groups = []
+        groups = []
+        spread_bias(0)
         for rows_sb, name in zip([x_rows[0]] + w3_rows + [x_rows[1]], ["x0", "w3_0", "w3_1", "w3_2", "x1"]):
             group = new_group(pools, rows_sb, WORDS_IN_HALVES, name)
             for j in range(group["n_tiles"]):
                 flip_row_tile(nc, pools, identity_f32, group, j)
-            quantise_group(nc, group)
-            first_groups.append(group)
-        x_groups = [first_groups[0], first_groups[-1]]
-        w3_groups = first_groups[1:-1]
+            if groups:
+                quantise_group(nc, groups[-1])
+            groups.append(group)
+            spread_bias(len(groups))
+        x_groups = [groups[0], groups[4]]
+        w3_groups = groups[1:4]
         w1_groups = []
 
         z_ps, z, norm, inverse, mu_flipped, mu_grouped = {}, {}, {}, {}, {}, {}
@@ -167,12 +187,12 @@ def tile_modelgraphpolicy_pb_kernel(tc, xum, action, up_w3, up_b3, dyn_w1_mu, dy
         def add_first_bias(i):
             z[i] = work.tile([P, MESSAGE], F32, tag="z", name="z")
             nc.vector.tensor_tensor(
-                out=z[i][:, 0:BANK], in0=z_ps[i][0][:], in1=b3_all[:, 0:BANK], op=ALU.add
+                out=z[i][:, 0:BANK], in0=z_ps[i][0][:], in1=bias_all[:, 0:BANK], op=ALU.add
             )
             nc.vector.tensor_tensor(
                 out=z[i][:, BANK:MESSAGE],
                 in0=z_ps[i][1][:, 0 : MESSAGE - BANK],
-                in1=b3_all[:, BANK:MESSAGE],
+                in1=bias_all[:, BANK:MESSAGE],
                 op=ALU.add,
             )
 
@@ -251,7 +271,7 @@ def tile_modelgraphpolicy_pb_kernel(tc, xum, action, up_w3, up_b3, dyn_w1_mu, dy
             nc.vector.tensor_tensor(
                 out=result[i][:, side * BANK : (side + 1) * BANK],
                 in0=acc[:],
-                in1=b1_all[:, n * BANK : (n + 1) * BANK],
+                in1=bias_all[:, B1_START + n * BANK : B1_START + (n + 1) * BANK],
                 op=ALU.add,
             )
             if side == 1:
@@ -267,18 +287,26 @@ def tile_modelgraphpolicy_pb_kernel(tc, xum, action, up_w3, up_b3, dyn_w1_mu, dy
                 else:
                     nc.scalar.activation(out=result[i][:], in_=result[i][:], func=ACT.Relu)
                 nc.sync.dma_start(
-                    out=out[i * P : (i + 1) * P, (n - 1) * BANK : (n + 1) * BANK], in_=result[i][:]
+                    out=out_tiles[i // GROUP, i % GROUP, :, (n - 1) * BANK : (n + 1) * BANK],
+                    in_=result[i][:],
                 )
 
         def bulk_quarter(step, quarter):
+            if step <= W1_GROUPS and quarter == 1:
+                quantise_group(nc, groups[-1])
             if step < W1_GROUPS:
                 if quarter == 0:
                     w1_groups.append(new_group(pools, w1_rows[step], WORDS_IN_TURN, "w1_%d" % step))
                 flip_row_tile(nc, pools, identity_f32, w1_groups[step], quarter)
                 if quarter == GROUP - 1:
-                    quantise_group(nc, w1_groups[step])
+                    groups.append(w1_groups[step])
             if step >= LAG:
                 second_matmul(step - LAG, quarter)
+
+        nc.vector.tensor_copy(
+            out=mu_planes[:, :, 1, :, message_p:P],
+            in_=action_sb[:].rearrange("b i (p t) -> b i t p", t=PACK),
+        )
 
         for step in range(B_TILES + LAG):
             link(invert_norm, step - 1)

import math
from contextlib import ExitStack

import concourse.mybir as mybir
from concourse.masks import make_identity

F32 = mybir.dt.float32
BF16 = mybir.dt.bfloat16
U32 = mybir.dt.uint32
U8 = mybir.dt.uint8
I32 = mybir.dt.int32
FP8X4 = mybir.dt.float8_e4m3fn_x4
ACT = mybir.ActivationFunctionType
ALU = mybir.AluOpType

P = 128
PACK = 4
PAIRS = 2
K = 1024
PASSES = K // (P * PACK)
BANK = 512

BATCH = 1024
MESSAGE = 896
ACTION = K - MESSAGE
OUT = 2048
EPS = 1e-12

B_TILES = BATCH // P
GROUP = BANK // P
W1_GROUPS = OUT // BANK
W3_GROUP_TILES = (4, 2, 1)
W3_GROUP_START = (0, 512, 768)

ROWS_APART = "(j r) k -> r j k"
ROWS_TOGETHER = "(r j) k -> r j k"

B1_START = 2 * BANK
BIAS_COLUMNS = B1_START + OUT

WORDS_IN_HALVES = "r (j g u p) -> r j g u p"
WORDS_IN_TURN = "r (j g p u) -> r j g u p"

LAG = W1_GROUPS

FLOPS = 2 * BATCH * K * (MESSAGE + OUT)


def load_rows(nc, pool, rows, row_order, name):
    n_tiles = rows.shape[0] // P
    rows_sb = pool.tile([P, n_tiles * K], BF16, name=name)
    nc.sync.dma_start(
        out=rows_sb[:].rearrange("r (j k) -> r j k", j=n_tiles),
        in_=rows.rearrange(row_order, r=P),
    )
    return rows_sb


def new_group(pools, rows_sb, word_order, name):
    n_rows = rows_sb.shape[1] // K * P
    grouped = pools["grouped"].tile([P, PASSES * n_rows * PACK], BF16, tag="grouped", align_bytes=64)
    return {
        "n_tiles": n_rows // P,
        "words": rows_sb[:].bitcast(F32).rearrange(word_order, j=n_rows // P, g=PASSES, u=PAIRS, p=P),
        "grouped": grouped,
        "grouped_words": grouped[:].bitcast(F32).rearrange("p (g r u) -> p g r u", g=PASSES, u=PAIRS),
        "codes": pools["operands"].tile([P, PASSES, n_rows], U32, name=name + "_codes", align_bytes=64),
        "scales": pools["operands"].tile([P, PASSES, n_rows], U8, name=name + "_scales", align_bytes=64),
    }


def flip_row_tile(nc, pools, identity, group, j):
    flipped = pools["psum"].tile([P, PASSES, PAIRS, P], F32, tag="bank")
    for g in range(PASSES):
        for u in range(PAIRS):
            nc.tensor.transpose(flipped[:, g, u, :], group["words"][:, j, g, u, :], identity[:])
    copy = nc.vector.tensor_copy if j == 1 else nc.scalar.copy
    copy(
        out=group["grouped_words"][:, :, j * P : (j + 1) * P, :],
        in_=flipped[:].rearrange("p g u r -> p g r u"),
    )


def quantise_group(nc, group):
    width = group["n_tiles"] * P * PACK
    for g in range(PASSES):
        nc.vector.quantize_mx(
            out=group["codes"][:, g, :].bitcast(FP8X4),
            scales=group["scales"][:, g, :],
            in_=group["grouped"][:, g * width : (g + 1) * width],
        )


def tile_modelgraphpolicy_pb_kernel(tc, xum, action, up_w3, up_b3, dyn_w1_mu, dyn_b1, out):
    nc = tc.nc
    with ExitStack() as ctx:
        const = ctx.enter_context(tc.tile_pool(name="const", bufs=1))
        raw = ctx.enter_context(tc.tile_pool(name="raw", bufs=1))
        work = ctx.enter_context(tc.tile_pool(name="work", bufs=3))
        small = ctx.enter_context(tc.tile_pool(name="small", bufs=3))
        results = ctx.enter_context(tc.tile_pool(name="results", bufs=6))
        pools = {
            "operands": ctx.enter_context(tc.tile_pool(name="operands", bufs=1)),
            "grouped": ctx.enter_context(tc.tile_pool(name="grouped", bufs=3)),
            "psum": ctx.enter_context(tc.psum_pool(name="psum", bufs=8)),
        }
        psum = pools["psum"]
        ctx.enter_context(tc.manual_schedule())

        bias_rows = const.tile([P, BIAS_COLUMNS], BF16)
        nc.vector.memset(bias_rows[:].bitcast(I32), 0)
        nc.scalar.dma_start(out=bias_rows[0:1, 0:MESSAGE], in_=up_b3.unsqueeze(0))
        nc.scalar.dma_start(out=bias_rows[0:1, B1_START:BIAS_COLUMNS], in_=dyn_b1.unsqueeze(0))
        x_rows = [load_rows(nc, raw, xum[0:BANK, :], ROWS_TOGETHER, "x_rows0")]
        w3_rows = [
            load_rows(nc, raw, up_w3[start : start + tiles * P, :], ROWS_APART, "w3_rows%d" % start)
            for start, tiles in zip(W3_GROUP_START, W3_GROUP_TILES)
        ]
        x_rows.append(load_rows(nc, raw, xum[BANK : 2 * BANK, :], ROWS_TOGETHER, "x_rows1"))
        action_sb = raw.tile([P, B_TILES, ACTION], BF16)
        nc.sync.dma_start(
            out=action_sb[:].rearrange("r (h j) a -> r h j a", j=GROUP),
            in_=action.rearrange("(h r j) a -> r h j a", r=P, j=GROUP),
        )
        w1_rows = [
            load_rows(nc, raw, dyn_w1_mu[n * BANK : (n + 1) * BANK, :], ROWS_APART, "w1_rows%d" % n)
            for n in range(W1_GROUPS)
        ]
        out_tiles = out.rearrange("(h r j) n -> h j r n", r=P, j=GROUP)

        identity_f32 = const.tile([P, P], F32)
        make_identity(nc, identity_f32[:])
        identity_bf16 = const.tile([P, P], BF16)
        make_identity(nc, identity_bf16[:])
        one = const.tile([P, 1], F32)
        nc.vector.memset(one[:], 1.0)
        nc.scalar.sqrt(one[:], one[:])

        ones = const.tile([P, P], BF16)
        nc.vector.memset(ones[:], 1.0)
        bias_all = const.tile([P, BIAS_COLUMNS], BF16)

        def spread_bias(piece):
            columns = slice(piece * BANK, (piece + 1) * BANK)
            spread = psum.tile([P, BANK], F32, tag="bank")
            nc.tensor.matmul(out=spread[:], lhsT=ones[:], rhs=bias_rows[:, columns], start=True, stop=True)
            nc.scalar.copy(out=bias_all[:, columns], in_=spread[:])

        mu_planes = raw.tile([P, B_TILES, PASSES, PACK, P], BF16)
        message_p = (MESSAGE - P * PACK) // PACK
        mu_codes = pools["operands"].tile([P, B_TILES, PASSES, P], U32, align_bytes=64)
        mu_scales = pools["operands"].tile([P, B_TILES, PASSES, P], U8, align_bytes=64)

        groups = []
        spread_bias(0)
        for rows_sb, name in zip([x_rows[0]] + w3_rows + [x_rows[1]], ["x0", "w3_0", "w3_1", "w3_2", "x1"]):
            group = new_group(pools, rows_sb, WORDS_IN_HALVES, name)
            for j in range(group["n_tiles"]):
                flip_row_tile(nc, pools, identity_f32, group, j)
            if groups:
                quantise_group(nc, groups[-1])
            groups.append(group)
            spread_bias(len(groups))
        x_groups = [groups[0], groups[4]]
        w3_groups = groups[1:4]
        w1_groups = []

        z_ps, z, norm, inverse, mu_flipped, mu_grouped = {}, {}, {}, {}, {}, {}

        def first_matmul(i):
            x = x_groups[i // GROUP]
            b_cols = slice((i % GROUP) * P, (i % GROUP + 1) * P)
            z_ps[i] = [psum.tile([P, BANK], F32, tag="bank", name="z_ps%d" % h) for h in range(2)]
            for w3, start in zip(w3_groups, W3_GROUP_START):
                width = w3["n_tiles"] * P
                for g in range(PASSES):
                    nc.tensor.matmul_mx(
                        out=z_ps[i][start // BANK][:, start % BANK : start % BANK + width],
                        lhsT=x["codes"][:, g, b_cols].bitcast(FP8X4),
                        lhsT_scale=x["scales"][:, g, b_cols],
                        rhs=w3["codes"][:, g, :].bitcast(FP8X4),
                        rhs_scale=w3["scales"][:, g, :],
                        start=(g == 0),
                        stop=(g == PASSES - 1),
                    )

        def add_first_bias(i):
            z[i] = work.tile([P, MESSAGE], F32, tag="z", name="z")
            nc.vector.tensor_tensor(
                out=z[i][:, 0:BANK], in0=z_ps[i][0][:], in1=bias_all[:, 0:BANK], op=ALU.add
            )
            nc.vector.tensor_tensor(
                out=z[i][:, BANK:MESSAGE],
                in0=z_ps[i][1][:, 0 : MESSAGE - BANK],
                in1=bias_all[:, BANK:MESSAGE],
                op=ALU.add,
            )

        def take_norm(i):
            squares = work.tile([P, MESSAGE], F32, tag="squares")
            sum_squares = small.tile([P, 1], F32, tag="sum_squares")
            nc.scalar.activation(out=squares[:], in_=z[i][:], func=ACT.Square, accum_out=sum_squares[:])
            norm[i] = small.tile([P, 1], F32, tag="norm", name="norm")
            nc.scalar.sqrt(norm[i][:], sum_squares[:])

        def invert_norm(i):
            floored = small.tile([P, 1], F32, tag="floored")
            nc.vector.tensor_scalar_max(floored[:], norm[i][:], EPS)
            inverse[i] = small.tile([P, 1], F32, tag="inverse", name="inverse")
            nc.vector.reciprocal(inverse[i][:], floored[:])

        def round_message(i):
            for g, first, last in ((0, 0, P * PACK), (1, P * PACK, MESSAGE)):
                planes = mu_planes[:, i, g, :, 0 : (last - first) // PACK].rearrange("b t p -> b p t")
                columns = z[i][:, first:last].rearrange("b (p t) -> b p t", t=PACK)
                if i < LAG:
                    nc.gpsimd.tensor_scalar(
                        out=planes,
                        in0=columns,
                        scalar1=inverse[i][:],
                        scalar2=0.0,
                        op0=ALU.mult,
                        op1=ALU.add,
                    )
                else:
                    nc.scalar.activation(out=planes, in_=columns, func=ACT.Copy, scale=inverse[i][:])

        def flip_mu(i):
            mu_flipped[i] = psum.tile([P, PASSES, PACK, P], BF16, tag="bank", name="mu_flipped")
            for g in range(PASSES):
                for t in range(PACK):
                    nc.tensor.transpose(
                        mu_flipped[i][:, g, t, :], mu_planes[:, i, g, t, :], identity_bf16[:]
                    )

        def group_mu(i):
            mu_grouped[i] = work.tile(
                [P, PASSES, P, PACK], BF16, tag="mu_grouped", name="mu_grouped", align_bytes=64
            )
            nc.scalar.copy(out=mu_grouped[i][:], in_=mu_flipped[i][:].rearrange("p g t b -> p g b t"))

        def quantise_mu(i):
            nc.vector.quantize_mx(
                out=mu_codes[:, i].rearrange("p g b -> p (g b)").bitcast(FP8X4),
                scales=mu_scales[:, i].rearrange("p g b -> p (g b)"),
                in_=mu_grouped[i][:].rearrange("p g b t -> p (g b t)"),
            )

        def link(stage, i):
            if 0 <= i < B_TILES:
                stage(i)

        result = {}

        def second_matmul(i, n):
            w1 = w1_groups[n]
            acc = psum.tile([P, BANK], F32, tag="bank")
            for g in range(PASSES):
                nc.tensor.matmul_mx(
                    out=acc[:],
                    lhsT=mu_codes[:, i, g, :].bitcast(FP8X4),
                    lhsT_scale=mu_scales[:, i, g, :],
                    rhs=w1["codes"][:, g, :].bitcast(FP8X4),
                    rhs_scale=w1["scales"][:, g, :],
                    start=(g == 0),
                    stop=(g == PASSES - 1),
                )
            side = n % 2
            if side == 0:
                result[i] = results.tile([P, 2 * BANK], F32, tag="result", name="result")
            nc.vector.tensor_tensor(
                out=result[i][:, side * BANK : (side + 1) * BANK],
                in0=acc[:],
                in1=bias_all[:, B1_START + n * BANK : B1_START + (n + 1) * BANK],
                op=ALU.add,
            )
            if side == 1:
                if i < LAG:
                    nc.gpsimd.tensor_scalar(
                        out=result[i][:],
                        in0=result[i][:],
                        scalar1=math.inf,
                        scalar2=0.0,
                        op0=ALU.min,
                        op1=ALU.max,
                    )
                else:
                    nc.scalar.activation(out=result[i][:], in_=result[i][:], func=ACT.Relu)
                nc.sync.dma_start(
                    out=out_tiles[i // GROUP, i % GROUP, :, (n - 1) * BANK : (n + 1) * BANK],
                    in_=result[i][:],
                )

        def bulk_quarter(step, quarter):
            if step <= W1_GROUPS and quarter == 1:
                quantise_group(nc, groups[-1])
            if step < W1_GROUPS:
                if quarter == 0:
                    w1_groups.append(new_group(pools, w1_rows[step], WORDS_IN_TURN, "w1_%d" % step))
                flip_row_tile(nc, pools, identity_f32, w1_groups[step], quarter)
                if quarter == GROUP - 1:
                    groups.append(w1_groups[step])
            if step >= LAG:
                second_matmul(step - LAG, quarter)

        nc.vector.tensor_copy(
            out=mu_planes[:, :, 1, :, message_p:P],
            in_=action_sb[:].rearrange("b i (p t) -> b i t p", t=PACK),
        )

        for step in range(B_TILES + LAG):
            link(invert_norm, step - 1)
            link(flip_mu, step - 2)
            link(first_matmul, step)
            bulk_quarter(step, 0)
            link(round_message, step - 1)
            link(add_first_bias, step)
            bulk_quarter(step, 1)
            link(group_mu, step - 2)
            link(quantise_mu, step - 3)
            bulk_quarter(step, 2)
            link(take_norm, step)
            bulk_quarter(step, 3)
